import numpy as np
import ml_dtypes


def mxq(x, axis, fmt="e4m3"):
    dtype, down = {"e4m3": (ml_dtypes.float8_e4m3fn, 7), "e5m2": (ml_dtypes.float8_e5m2, 14)}[fmt]
    v = np.moveaxis(np.asarray(x, np.float32).astype(ml_dtypes.bfloat16).astype(np.float64), axis, -1)
    blocks = v.reshape(v.shape[:-1] + (-1, 32))
    amax = np.abs(blocks).max(-1, keepdims=True)
    byte = np.maximum(np.where(amax > 0, np.frexp(amax)[1] - 1 + 127, 0) - down, 1)
    scale = np.exp2(byte - 127.0)
    codes = (blocks / scale).astype(np.float32).astype(dtype).astype(np.float64)
    return np.moveaxis((codes * scale).reshape(v.shape), -1, axis)


WIDE = False


def mx_kscale(k):
    if not WIDE:
        return np.ones(k)
    levels = np.array([10, -10, 5, -5, 0])
    if k % 512:
        return np.exp2(np.random.permutation(np.resize(levels, k // 32))).repeat(32)
    a = np.empty((k // 512, 16))
    for p in range(k // 512):
        a[p, :8] = np.random.permutation(np.resize(levels, 8))
        for g in range(8):
            far = levels[np.abs(levels - a[p, g]) >= 10]
            a[p, g + 8] = far[np.random.randint(len(far))]
    return np.exp2(a.ravel()).repeat(32)


BF16 = ml_dtypes.bfloat16


def bf(x):
    return np.asarray(x, np.float32).astype(BF16)


def f64(x):
    return np.asarray(x).astype(np.float64)


B, H, D, DV, N = 1, 1, 512, 1024, 4096
DIM = H * DV


def setup_inputs():
    s, t = mx_kscale(N), mx_kscale(D)
    c = np.exp2(np.round(np.log2(s.mean())))
    q = (np.random.standard_normal((B, H, D, N)) - 1.0) * 3.0 / np.sqrt(D) / t[:, None]
    k = (np.random.standard_normal((B, H, D, N)) - 1.0) * 3.0 / np.sqrt(N) * t[:, None] * s
    v = np.random.standard_normal((B, H, DV, N)) * 0.125 * np.sqrt(N) * c / s
    return {"q": bf(q), "k": bf(k), "v": bf(v)}


def reference(q, k, v):
    qr = np.maximum(f64(q), 0.0)
    kr = np.maximum(f64(k), 0.0)
    vk = mxq(f64(v), 3, "e4m3") @ mxq(kr, 3, "e4m3").transpose(0, 1, 3, 2)
    ksum = kr.sum(-1)
    num = mxq(vk, 3, "e4m3") @ mxq(qr, 2, "e4m3")
    den = (ksum[..., None] * qr).sum(-2, keepdims=True)
    out = num / den
    return out.transpose(0, 2, 1, 3).reshape(B, -1, DIM)

@@ -1,0 +1,361 @@
+from contextlib import ExitStack
+
+import concourse.mybir as mybir
+from concourse.masks import make_identity
+
+F32 = mybir.dt.float32
+BF16 = mybir.dt.bfloat16
+U32 = mybir.dt.uint32
+U8 = mybir.dt.uint8
+FP8X4 = mybir.dt.float8_e4m3fn_x4
+ALU = mybir.AluOpType
+AXIS = mybir.AxisListType
+
+P = 128
+PACK = 4
+K_PASS = P * PACK
+E = 512
+DV = 1024
+N = 4096
+E_TILES = E // P
+D_TILES = DV // P
+TOKEN_PASSES = N // K_PASS
+PAIR = 2
+PASS_WORDS = K_PASS // PAIR
+BANK_PASSES = 2
+N_TILE = 512
+K_PARTS = 2
+K_PART = N // K_PARTS
+Q_RANGES = 4
+RANGE = N // Q_RANGES
+RANGE_TILES = RANGE // P
+RANGE_BANKS = RANGE // N_TILE
+RUN = 4
+STATE_PASSES = E_TILES * TOKEN_PASSES
+STEPS = 8
+KSUM_PIECES = 3
+DEN_COLS = 32
+
+V_BUFS = 6
+GROUPED_BUFS = 3
+V_MX_BUFS = 2
+VK_BUFS = 2
+REP_BUFS = 2
+BANKS = 7
+STAGING_BUFS = 8
+
+FIRST_ROUND = -E_TILES
+FIRST_STATE_ROUND = -1
+LAST_ROUND = D_TILES
+
+FLOPS = 2 * DV * E * N * 2 + 2 * E * N
+
+
+def tile_relu_linear_att_pa_t_kernel(tc, q, k, v, out):
+    nc = tc.nc
+    q_rows = q.rearrange("b h e n -> (b h e) n")
+    k_rows = k.rearrange("b h e n -> (b h e) n")
+    v_rows = v.rearrange("b h d n -> (b h d) n")
+    out_rows = out.rearrange("b (d x) c -> (b d) (x c)", x=N // DV)
+
+    with ExitStack() as ctx:
+        ctx.enter_context(tc.manual_schedule())
+        keep = ctx.enter_context(tc.tile_pool(name="keep", bufs=1))
+        v_in = ctx.enter_context(tc.tile_pool(name="v_in", bufs=V_BUFS))
+        grouped_pool = ctx.enter_context(tc.tile_pool(name="grouped", bufs=GROUPED_BUFS))
+        v_mx = ctx.enter_context(tc.tile_pool(name="v_mx", bufs=V_MX_BUFS))
+        vk_pool = ctx.enter_context(tc.tile_pool(name="vk", bufs=VK_BUFS))
+        rep_pool = ctx.enter_context(tc.tile_pool(name="rep", bufs=REP_BUFS))
+        psum = ctx.enter_context(tc.psum_pool(name="psum", bufs=1))
+
+        ident_f32 = keep.tile([P, P], F32)
+        make_identity(nc, ident_f32[:])
+
+        k_codes = keep.tile([P, TOKEN_PASSES * E], U32, align_bytes=64)
+        k_scales = keep.tile([P, TOKEN_PASSES * E], U8, align_bytes=64)
+        q_codes = keep.tile([P, N], U32, align_bytes=64)
+        q_scales = keep.tile([P, N], U8, align_bytes=64)
+        vk_codes = keep.tile([P, DV], U32, align_bytes=64)
+        vk_scales = keep.tile([P, DV], U8, align_bytes=64)
+        q_ranges = [keep.tile([P, E_TILES, RANGE], BF16, name="q_sb%d" % r) for r in range(Q_RANGES)]
+        rden_all = keep.tile([P, N], F32)
+        ksum_parts = keep.tile([P, E_TILES, K_PARTS], F32)
+        ksum = keep.tile([P, E_TILES], F32)
+        pieces = keep.tile([P, E_TILES, DEN_COLS], BF16)
+        rest1 = keep.tile([P, E_TILES], F32)
+        rest2 = keep.tile([P, E_TILES], F32)
+        den = keep.tile([P, Q_RANGES, RANGE_TILES], F32)
+        rden = keep.tile([P, Q_RANGES, RANGE_TILES], F32)
+
+        def new_bank(shape):
+            return psum.tile(shape, F32, tag="bank", bufs=BANKS, name="bank")
+
+        def tokens_to_partitions(rows):
+            words = rows[:].bitcast(F32)
+            grouped = grouped_pool.tile([P, PACK * TOKEN_PASSES * P], BF16, tag="grouped", align_bytes=64)
+            grouped_words = grouped[:].bitcast(F32).rearrange("p (g d u) -> p g d u", g=TOKEN_PASSES, u=PAIR)
+            for first_pass in range(0, TOKEN_PASSES, BANK_PASSES):
+                bank = new_bank([P, BANK_PASSES, PAIR, P])
+                for g in range(BANK_PASSES):
+                    for u in range(PAIR):
+                        w0 = (first_pass + g) * PASS_WORDS
+                        nc.tensor.transpose(
+                            bank[:, g, u, :], words[:, w0 + u : w0 + PASS_WORDS : PAIR], ident_f32[:]
+                        )
+                nc.scalar.copy(
+                    out=grouped_words[:, first_pass : first_pass + BANK_PASSES, :, :],
+                    in_=bank[:].rearrange("p g u d -> p g d u"),
+                )
+            return grouped
+
+        v_tiles = {}
+        v_grouped = {}
+        v_quantised = {}
+        vk_sums = {}
+        vk_rounded = {}
+
+        def load_v(m):
+            v_sb = v_in.tile([P, N], BF16, name="v_sb")
+            nc.sync.dma_start(out=v_sb[:], in_=v_rows[m * P : (m + 1) * P, :])
+            v_tiles[m] = v_sb
+
+        def transpose_v(m):
+            v_grouped[m] = tokens_to_partitions(v_tiles[m])
+
+        def quantise_v(m):
+            codes = v_mx.tile([P, TOKEN_PASSES * P], U32, tag="v_codes", align_bytes=64)
+            scales = v_mx.tile([P, TOKEN_PASSES * P], U8, tag="v_scales", align_bytes=64)
+            nc.vector.quantize_mx(out=codes[:].bitcast(FP8X4), scales=scales[:], in_=v_grouped[m][:])
+            v_quantised[m] = (codes, scales)
+
+        def state_pass(m, i):
+            t = i // TOKEN_PASSES
+            g = i % TOKEN_PASSES
+            if i == 0:
+                vk_sums[m] = psum.tile([P, E_TILES, P], F32, tag="vk_ps", bufs=1, name="vk_ps")
+            codes, scales = v_quantised[m]
+            e_cols = slice((t * TOKEN_PASSES + g) * P, (t * TOKEN_PASSES + g + 1) * P)
+            nc.tensor.matmul_mx(
+                out=vk_sums[m][:, t, :],
+                lhsT=k_codes[:, e_cols].bitcast(FP8X4),
+                lhsT_scale=k_scales[:, e_cols],
+                rhs=codes[:, g * P : (g + 1) * P].bitcast(FP8X4),
+                rhs_scale=scales[:, g * P : (g + 1) * P],
+                start=(g == 0),
+                stop=(g == TOKEN_PASSES - 1),
+            )
+
+        def round_state(m):
+            vk_grouped = vk_pool.tile([P, P, PACK], BF16, tag="vk_grouped", align_bytes=64)
+            nc.scalar.copy(out=vk_grouped[:], in_=vk_sums[m][:].rearrange("p t d -> p d t"))
+            vk_rounded[m] = vk_grouped
+
+        def quantise_state(m):
+            cols = slice(m * P, (m + 1) * P)
+            nc.vector.quantize_mx(
+                out=vk_codes[:, cols].bitcast(FP8X4),
+                scales=vk_scales[:, cols],
+                in_=vk_rounded[m][:].rearrange("p d t -> p (d t)"),
+            )
+
+        q_grouped = {}
+        den_sums = {}
+        repeated = {}
+
+        def load_q(r):
+            nc.sync.dma_start(
+                out=q_ranges[r][:],
+                in_=q_rows.rearrange("(p t) n -> p t n", t=PACK)[:, :, r * RANGE : (r + 1) * RANGE],
+            )
+
+        def relu_q(r):
+            nc.vector.tensor_scalar_max(out=q_ranges[r][:], in0=q_ranges[r][:], scalar1=0.0)
+
+        def regroup_q(r):
+            grouped = grouped_pool.tile([P, PACK * RANGE], BF16, tag="grouped", align_bytes=64)
+            half = RANGE // 2
+            for side in range(2):
+                dst = grouped[:, side * PACK * half : (side + 1) * PACK * half].rearrange(
+                    "p (c i t) -> p c t i", i=RUN, t=PACK
+                )
+                src = q_ranges[r][:, :, side * half : (side + 1) * half].rearrange("p t (c i) -> p c t i", i=RUN)
+                if side == 0:
+                    nc.vector.tensor_copy(out=dst, in_=src)
+                else:
+                    nc.scalar.copy(out=dst, in_=src)
+            q_grouped[r] = grouped
+
+        def quantise_q(r):
+            cols = slice(r * RANGE, (r + 1) * RANGE)
+            nc.vector.quantize_mx(out=q_codes[:, cols].bitcast(FP8X4), scales=q_scales[:, cols], in_=q_grouped[r][:])
+
+        def den_matmuls(r):
+            den_ps = new_bank([P, RANGE_TILES, DEN_COLS])
+            for j in range(RANGE_TILES):
+                for t in range(E_TILES):
+                    nc.tensor.matmul(
+                        out=den_ps[:, j, :],
+                        lhsT=q_ranges[r][:, t, j * P : (j + 1) * P],
+                        rhs=pieces[:, t, :],
+                        start=(t == 0),
+                        stop=(t == E_TILES - 1),
+                    )
+            den_sums[r] = den_ps
+
+        def reciprocal_den(r):
+            nc.vector.tensor_reduce(out=den[:, r, :], in_=den_sums[r][:, :, 0:KSUM_PIECES], axis=AXIS.X, op=ALU.add)
+            nc.vector.reciprocal(out=rden[:, r, :], in_=den[:, r, :])
+            rep = rep_pool.tile([P, RANGE_TILES, P], F32)
+            nc.gpsimd.tensor_scalar(
+                out=rep[:],
+                in0=rden[:, r, :].unsqueeze(2).to_broadcast([P, RANGE_TILES, P]),
+                scalar1=1.0,
+                scalar2=0.0,
+                op0=ALU.mult,
+                op1=ALU.add,
+            )
+            repeated[r] = rep
+
+        def spread_den(r):
+            for h in range(RANGE_BANKS):
+                bank = new_bank([P, N_TILE // P, P])
+                for square in range(N_TILE // P):
+                    nc.tensor.transpose(
+                        bank[:, square, :], repeated[r][:, h * (N_TILE // P) + square, :], ident_f32[:]
+                    )
+                first = r * RANGE + h * N_TILE
+                nc.scalar.copy(out=rden_all[:, first : first + N_TILE], in_=bank[:].rearrange("p i c -> p (i c)"))
+
+        k_tiles = {}
+        k_grouped = {}
+
+        def prepare_k(t):
+            kr = k_tiles[t]
+            for c in range(K_PARTS):
+                nc.vector.tensor_scalar(
+                    out=kr[:, c * K_PART : (c + 1) * K_PART],
+                    in0=kr[:, c * K_PART : (c + 1) * K_PART],
+                    scalar1=0.0,
+                    scalar2=None,
+                    op0=ALU.max,
+                    op1=ALU.add,
+                    accum_out=ksum_parts[:, t, c : c + 1],
+                )
+            k_grouped[t] = tokens_to_partitions(kr)
+
+        def quantise_k(t):
+            cols = slice(t * TOKEN_PASSES * P, (t + 1) * TOKEN_PASSES * P)
+            nc.vector.quantize_mx(out=k_codes[:, cols].bitcast(FP8X4), scales=k_scales[:, cols], in_=k_grouped[t][:])
+
+        def split_ksum():
+            nc.vector.tensor_reduce(out=ksum[:], in_=ksum_parts[:], axis=AXIS.X, op=ALU.add)
+            nc.vector.memset(pieces[:], 0.0)
+            nc.vector.tensor_copy(out=pieces[:, :, 0], in_=ksum[:])
+            nc.vector.tensor_sub(out=rest1[:], in0=ksum[:], in1=pieces[:, :, 0])
+            nc.vector.tensor_copy(out=pieces[:, :, 1], in_=rest1[:])
+            nc.vector.tensor_sub(out=rest2[:], in0=rest1[:], in1=pieces[:, :, 1])
+            nc.vector.tensor_copy(out=pieces[:, :, 2], in_=rest2[:])
+
+        results = {}
+
+        def output_pass(m, r, h):
+            if h == 0:
+                results[(m, r)] = staging.tile([P, RANGE], F32, tag="result", name="result")
+            d_cols = slice(m * P, (m + 1) * P)
+            n_cols = slice(r * RANGE + h * N_TILE, r * RANGE + (h + 1) * N_TILE)
+            num = new_bank([P, N_TILE])
+            nc.tensor.matmul_mx(
+                out=num[:],
+                lhsT=vk_codes[:, d_cols].bitcast(FP8X4),
+                lhsT_scale=vk_scales[:, d_cols],
+                rhs=q_codes[:, n_cols].bitcast(FP8X4),
+                rhs_scale=q_scales[:, n_cols],
+                start=True,
+                stop=True,
+            )
+            part = results[(m, r)][:, h * N_TILE : (h + 1) * N_TILE]
+            if (RANGE_BANKS * (m + r) + h) % 3 == 1:
+                nc.scalar.copy(out=part, in_=num[:])
+                nc.gpsimd.tensor_mul(out=part, in0=part, in1=rden_all[:, n_cols])
+            else:
+                nc.vector.tensor_mul(out=part, in0=num[:], in1=rden_all[:, n_cols])
+            if h == RANGE_BANKS - 1:
+                nc.sync.dma_start(out=out_rows[d_cols, r * RANGE : (r + 1) * RANGE], in_=results[(m, r)][:])
+
+        def is_k_tile(t):
+            return 0 <= t < E_TILES
+
+        def is_tile(m):
+            return 0 <= m < D_TILES
+
+        def is_range(r):
+            return 0 <= r < Q_RANGES
+
+        def work_round(p):
+            if is_k_tile(p + E_TILES):
+                prepare_k(p + E_TILES)
+            if is_k_tile(p + E_TILES - 1) and p + E_TILES - 1 != E_TILES - 1:
+                quantise_k(p + E_TILES - 1)
+            if is_tile(p + 2):
+                transpose_v(p + 2)
+                if p + 2 + V_BUFS < D_TILES:
+                    load_v(p + 2 + V_BUFS)
+            if is_range(p - 1):
+                spread_den(p - 1)
+            if p == FIRST_STATE_ROUND:
+                quantise_v(0)
+                quantise_k(E_TILES - 1)
+            if p == FIRST_STATE_ROUND + 1:
+                split_ksum()
+            if is_range(p):
+                regroup_q(p)
+            if is_range(p + 1):
+                relu_q(p + 1)
+            if is_tile(p):
+                quantise_state(p)
+            if is_range(p):
+                den_matmuls(p)
+                reciprocal_den(p)
+            blocks = []
+            if is_range(p - 1):
+                blocks = blocks + [(m, p - 1) for m in range(p - 1)]
+            if is_tile(p - 1):
+                blocks = blocks + [(p - 1, r) for r in range(min(p, Q_RANGES))]
+            passes = [(m, r, h) for m, r in blocks for h in range(RANGE_BANKS)]
+            share = (len(passes) + STEPS - 1) // STEPS
+            if is_tile(p + 1):
+                for s in range(STEPS):
+                    for i in range(s * STATE_PASSES // STEPS, (s + 1) * STATE_PASSES // STEPS):
+                        state_pass(p + 1, i)
+                    for m, r, h in passes[share * s : share * (s + 1)]:
+                        output_pass(m, r, h)
+                    if s == STEPS // 2 - 1 and is_tile(p + 2):
+                        quantise_v(p + 2)
+                round_state(p + 1)
+            else:
+                for m, r, h in passes:
+                    output_pass(m, r, h)
+            if is_range(p):
+                quantise_q(p)
+
+        with tc.tile_pool(name="k_in", bufs=E_TILES) as k_in:
+            for t in range(E_TILES):
+                k_tiles[t] = k_in.tile([P, N], BF16, name="k_sb")
+                for c in range(K_PARTS):
+                    nc.sync.dma_start(
+                        out=k_tiles[t][:, c * K_PART : (c + 1) * K_PART],
+                        in_=k_rows.rearrange("(p t) n -> t p n", t=PACK)[t, :, c * K_PART : (c + 1) * K_PART],
+                    )
+            load_v(0)
+            load_v(1)
+            load_q(0)
+            for r in range(1, Q_RANGES):
+                load_q(r)
+                load_v(r + 1)
+            for m in range(Q_RANGES + 1, V_BUFS):
+                load_v(m)
+            for p in range(FIRST_ROUND, 0):
+                work_round(p)
+        staging = ctx.enter_context(tc.tile_pool(name="staging", bufs=STAGING_BUFS))
+        for p in range(0, LAST_ROUND + 1):
+            work_round(p)

@@ -26,6 +26,7 @@ BANK_PASSES = 2
 N_TILE = 512
 K_PARTS = 2
 K_PART = N // K_PARTS
+PART_PASSES = TOKEN_PASSES // K_PARTS
 Q_RANGES = 4
 RANGE = N // Q_RANGES
 RANGE_TILES = RANGE // P
@@ -90,7 +91,7 @@ def tile_relu_linear_att_pa_t_kernel(tc, q, k, v, out):
         def new_bank(shape):
             return psum.tile(shape, F32, tag="bank", bufs=BANKS, name="bank")
 
-        def tokens_to_partitions(rows):
+        def tokens_to_partitions(rows, split):
             words = rows[:].bitcast(F32)
             grouped = grouped_pool.tile([P, PACK * TOKEN_PASSES * P], BF16, tag="grouped", align_bytes=64)
             grouped_words = grouped[:].bitcast(F32).rearrange("p (g d u) -> p g d u", g=TOKEN_PASSES, u=PAIR)
@@ -98,10 +99,14 @@ def tile_relu_linear_att_pa_t_kernel(tc, q, k, v, out):
                 bank = new_bank([P, BANK_PASSES, PAIR, P])
                 for g in range(BANK_PASSES):
                     for u in range(PAIR):
-                        w0 = (first_pass + g) * PASS_WORDS
-                        nc.tensor.transpose(
-                            bank[:, g, u, :], words[:, w0 + u : w0 + PASS_WORDS : PAIR], ident_f32[:]
-                        )
+                        if split:
+                            part, g_part = divmod(first_pass + g, PART_PASSES)
+                            w0 = (part * PAIR + u) * PART_PASSES * P + g_part * P
+                            cols = slice(w0, w0 + P)
+                        else:
+                            w0 = (first_pass + g) * PASS_WORDS
+                            cols = slice(w0 + u, w0 + PASS_WORDS, PAIR)
+                        nc.tensor.transpose(bank[:, g, u, :], words[:, cols], ident_f32[:])
                 nc.scalar.copy(
                     out=grouped_words[:, first_pass : first_pass + BANK_PASSES, :, :],
                     in_=bank[:].rearrange("p g u d -> p g d u"),
@@ -120,7 +125,7 @@ def tile_relu_linear_att_pa_t_kernel(tc, q, k, v, out):
             v_tiles[m] = v_sb
 
         def transpose_v(m):
-            v_grouped[m] = tokens_to_partitions(v_tiles[m])
+            v_grouped[m] = tokens_to_partitions(v_tiles[m], False)
 
         def quantise_v(m):
             codes = v_mx.tile([P, TOKEN_PASSES * P], U32, tag="v_codes", align_bytes=64)
@@ -230,18 +235,19 @@ def tile_relu_linear_att_pa_t_kernel(tc, q, k, v, out):
         k_grouped = {}
 
         def prepare_k(t):
-            kr = k_tiles[t]
+            kr = kr_pool.tile([P, N], BF16, name="kr")
             for c in range(K_PARTS):
+                part = slice(c * K_PART, (c + 1) * K_PART)
                 nc.vector.tensor_scalar(
-                    out=kr[:, c * K_PART : (c + 1) * K_PART],
-                    in0=kr[:, c * K_PART : (c + 1) * K_PART],
+                    out=kr[:, part].rearrange("p (u w y) -> p u w y", u=PAIR, y=PAIR),
+                    in0=k_tiles[t][:, part].rearrange("p (w u y) -> p u w y", u=PAIR, y=PAIR),
                     scalar1=0.0,
                     scalar2=None,
                     op0=ALU.max,
                     op1=ALU.add,
                     accum_out=ksum_parts[:, t, c : c + 1],
                 )
-            k_grouped[t] = tokens_to_partitions(kr)
+            k_grouped[t] = tokens_to_partitions(kr, True)
 
         def quantise_k(t):
             cols = slice(t * TOKEN_PASSES * P, (t + 1) * TOKEN_PASSES * P)
@@ -338,7 +344,7 @@ def tile_relu_linear_att_pa_t_kernel(tc, q, k, v, out):
             if is_range(p):
                 quantise_q(p)
 
-        with tc.tile_pool(name="k_in", bufs=E_TILES) as k_in:
+        with tc.tile_pool(name="k_in", bufs=3) as k_in, tc.tile_pool(name="kr", bufs=2) as kr_pool:
             for t in range(E_TILES):
                 k_tiles[t] = k_in.tile([P, N], BF16, name="k_sb")
                 for c in range(K_PARTS):

@@ -24,6 +24,7 @@ PAIR = 2
 PASS_WORDS = K_PASS // PAIR
 BANK_PASSES = 2
 N_TILE = 512
+GROUPS = N_TILE // P
 K_PARTS = 2
 K_PART = N // K_PARTS
 PART_PASSES = TOKEN_PASSES // K_PARTS
@@ -41,7 +42,6 @@ V_BUFS = 6
 GROUPED_BUFS = 3
 V_MX_BUFS = 2
 VK_BUFS = 2
-REP_BUFS = 2
 BANKS = 7
 STAGING_BUFS = 8
 
@@ -66,7 +66,6 @@ def tile_relu_linear_att_pa_t_kernel(tc, q, k, v, out):
         grouped_pool = ctx.enter_context(tc.tile_pool(name="grouped", bufs=GROUPED_BUFS))
         v_mx = ctx.enter_context(tc.tile_pool(name="v_mx", bufs=V_MX_BUFS))
         vk_pool = ctx.enter_context(tc.tile_pool(name="vk", bufs=VK_BUFS))
-        rep_pool = ctx.enter_context(tc.tile_pool(name="rep", bufs=REP_BUFS))
         psum = ctx.enter_context(tc.psum_pool(name="psum", bufs=1))
 
         ident_f32 = keep.tile([P, P], F32)
@@ -165,7 +164,6 @@ def tile_relu_linear_att_pa_t_kernel(tc, q, k, v, out):
 
         q_grouped = {}
         den_sums = {}
-        repeated = {}
 
         def load_q(r):
             nc.sync.dma_start(
@@ -197,10 +195,11 @@ def tile_relu_linear_att_pa_t_kernel(tc, q, k, v, out):
         def den_matmuls(r):
             den_ps = new_bank([P, RANGE_TILES, DEN_COLS])
             for j in range(RANGE_TILES):
+                h, i = divmod(j, GROUPS)
                 for t in range(E_TILES):
                     nc.tensor.matmul(
                         out=den_ps[:, j, :],
-                        lhsT=q_ranges[r][:, t, j * P : (j + 1) * P],
+                        lhsT=q_ranges[r][:, t, h * N_TILE + i : (h + 1) * N_TILE : GROUPS],
                         rhs=pieces[:, t, :],
                         start=(t == 0),
                         stop=(t == E_TILES - 1),
@@ -210,26 +209,18 @@ def tile_relu_linear_att_pa_t_kernel(tc, q, k, v, out):
         def reciprocal_den(r):
             nc.vector.tensor_reduce(out=den[:, r, :], in_=den_sums[r][:, :, 0:KSUM_PIECES], axis=AXIS.X, op=ALU.add)
             nc.vector.reciprocal(out=rden[:, r, :], in_=den[:, r, :])
-            rep = rep_pool.tile([P, RANGE_TILES, P], F32)
-            nc.gpsimd.tensor_scalar(
-                out=rep[:],
-                in0=rden[:, r, :].unsqueeze(2).to_broadcast([P, RANGE_TILES, P]),
-                scalar1=1.0,
-                scalar2=0.0,
-                op0=ALU.mult,
-                op1=ALU.add,
-            )
-            repeated[r] = rep
 
         def spread_den(r):
             for h in range(RANGE_BANKS):
                 bank = new_bank([P, N_TILE // P, P])
                 for square in range(N_TILE // P):
+                    j = h * (N_TILE // P) + square
                     nc.tensor.transpose(
-                        bank[:, square, :], repeated[r][:, h * (N_TILE // P) + square, :], ident_f32[:]
+                        bank[:, square, :], rden[:, r, j : j + 1].to_broadcast([P, P]), ident_f32[:]
                     )
                 first = r * RANGE + h * N_TILE
-                nc.scalar.copy(out=rden_all[:, first : first + N_TILE], in_=bank[:].rearrange("p i c -> p (i c)"))
+                spread = rden_all[:, first : first + N_TILE].rearrange("p (n i) -> p n i", i=GROUPS)
+                nc.scalar.copy(out=spread, in_=bank[:].rearrange("p i n -> p n i"))
 
         k_tiles = {}
         k_grouped = {}

@@ -24,7 +24,6 @@ PAIR = 2
 PASS_WORDS = K_PASS // PAIR
 BANK_PASSES = 2
 N_TILE = 512
-GROUPS = N_TILE // P
 K_PARTS = 2
 K_PART = N // K_PARTS
 PART_PASSES = TOKEN_PASSES // K_PARTS
@@ -45,9 +44,17 @@ VK_BUFS = 2
 BANKS = 7
 STAGING_BUFS = 8
 
+V_QUANTISE_STEP = 3
+V_SPLIT_STEP = 2
+DEN_STEP = 5
+Q_QUANTISE_STEP = 7
+CARRY = 4
+CARRY_FROM = 3
+FIRST_SPLIT = 3
+LOADS = "k0 k1 k2 v0 k3 v1 v2 q0 v3 q1 v4 q2 q3 v5"
 FIRST_ROUND = -E_TILES
 FIRST_STATE_ROUND = -1
-LAST_ROUND = D_TILES
+LAST_ROUND = D_TILES - 1
 
 FLOPS = 2 * DV * E * N * 2 + 2 * E * N
 
@@ -65,6 +72,7 @@ def tile_relu_linear_att_pa_t_kernel(tc, q, k, v, out):
         v_in = ctx.enter_context(tc.tile_pool(name="v_in", bufs=V_BUFS))
         grouped_pool = ctx.enter_context(tc.tile_pool(name="grouped", bufs=GROUPED_BUFS))
         v_mx = ctx.enter_context(tc.tile_pool(name="v_mx", bufs=V_MX_BUFS))
+        split_pool = ctx.enter_context(tc.tile_pool(name="split", bufs=2))
         vk_pool = ctx.enter_context(tc.tile_pool(name="vk", bufs=VK_BUFS))
         psum = ctx.enter_context(tc.psum_pool(name="psum", bufs=1))
 
@@ -112,6 +120,8 @@ def tile_relu_linear_att_pa_t_kernel(tc, q, k, v, out):
                 )
             return grouped
 
+        nc.vector.memset(pieces[:], 0.0)
+
         v_tiles = {}
         v_grouped = {}
         v_quantised = {}
@@ -123,8 +133,19 @@ def tile_relu_linear_att_pa_t_kernel(tc, q, k, v, out):
             nc.sync.dma_start(out=v_sb[:], in_=v_rows[m * P : (m + 1) * P, :])
             v_tiles[m] = v_sb
 
+        def split_v(m):
+            v_sb = v_tiles[m]
+            v_split = split_pool.tile([P, N], BF16, name="v_split")
+            for c in range(K_PARTS):
+                part = slice(c * (N // PAIR) // K_PARTS, (c + 1) * (N // PAIR) // K_PARTS)
+                nc.scalar.copy(
+                    out=v_split[:].bitcast(F32)[:, part].rearrange("p (u w) -> p u w", u=PAIR),
+                    in_=v_sb[:].bitcast(F32)[:, part].rearrange("p (w u) -> p u w", u=PAIR),
+                )
+            v_tiles[m] = v_split
+
         def transpose_v(m):
-            v_grouped[m] = tokens_to_partitions(v_tiles[m], False)
+            v_grouped[m] = tokens_to_partitions(v_tiles[m], m >= FIRST_SPLIT)
 
         def quantise_v(m):
             codes = v_mx.tile([P, TOKEN_PASSES * P], U32, tag="v_codes", align_bytes=64)
@@ -171,21 +192,13 @@ def tile_relu_linear_att_pa_t_kernel(tc, q, k, v, out):
                 in_=q_rows.rearrange("(p t) n -> p t n", t=PACK)[:, :, r * RANGE : (r + 1) * RANGE],
             )
 
-        def relu_q(r):
-            nc.vector.tensor_scalar_max(out=q_ranges[r][:], in0=q_ranges[r][:], scalar1=0.0)
-
         def regroup_q(r):
             grouped = grouped_pool.tile([P, PACK * RANGE], BF16, tag="grouped", align_bytes=64)
-            half = RANGE // 2
-            for side in range(2):
-                dst = grouped[:, side * PACK * half : (side + 1) * PACK * half].rearrange(
-                    "p (c i t) -> p c t i", i=RUN, t=PACK
-                )
-                src = q_ranges[r][:, :, side * half : (side + 1) * half].rearrange("p t (c i) -> p c t i", i=RUN)
-                if side == 0:
-                    nc.vector.tensor_copy(out=dst, in_=src)
-                else:
-                    nc.scalar.copy(out=dst, in_=src)
+            nc.vector.tensor_scalar_max(
+                out=grouped[:].rearrange("p (c i t) -> p c t i", i=RUN, t=PACK),
+                in0=q_ranges[r][:].rearrange("p t (c i) -> p c t i", i=RUN),
+                scalar1=0.0,
+            )
             q_grouped[r] = grouped
 
         def quantise_q(r):
@@ -194,12 +207,12 @@ def tile_relu_linear_att_pa_t_kernel(tc, q, k, v, out):
 
         def den_matmuls(r):
             den_ps = new_bank([P, RANGE_TILES, DEN_COLS])
+            grouped = q_grouped[r][:].rearrange("p (n t) -> p n t", t=PACK)
             for j in range(RANGE_TILES):
-                h, i = divmod(j, GROUPS)
                 for t in range(E_TILES):
                     nc.tensor.matmul(
                         out=den_ps[:, j, :],
-                        lhsT=q_ranges[r][:, t, h * N_TILE + i : (h + 1) * N_TILE : GROUPS],
+                        lhsT=grouped[:, j * P : (j + 1) * P, t],
                         rhs=pieces[:, t, :],
                         start=(t == 0),
                         stop=(t == E_TILES - 1),
@@ -219,11 +232,18 @@ def tile_relu_linear_att_pa_t_kernel(tc, q, k, v, out):
                         bank[:, square, :], rden[:, r, j : j + 1].to_broadcast([P, P]), ident_f32[:]
                     )
                 first = r * RANGE + h * N_TILE
-                spread = rden_all[:, first : first + N_TILE].rearrange("p (n i) -> p n i", i=GROUPS)
-                nc.scalar.copy(out=spread, in_=bank[:].rearrange("p i n -> p n i"))
+                nc.scalar.copy(out=rden_all[:, first : first + N_TILE], in_=bank[:].rearrange("p i c -> p (i c)"))
 
         k_tiles = {}
         k_grouped = {}
+
+        def load_k(t, k_in):
+            k_tiles[t] = k_in.tile([P, N], BF16, name="k_sb")
+            for c in range(K_PARTS):
+                nc.sync.dma_start(
+                    out=k_tiles[t][:, c * K_PART : (c + 1) * K_PART],
+                    in_=k_rows.rearrange("(p t) n -> t p n", t=PACK)[t, :, c * K_PART : (c + 1) * K_PART],
+                )
 
         def prepare_k(t):
             kr = kr_pool.tile([P, N], BF16, name="kr")
@@ -246,7 +266,6 @@ def tile_relu_linear_att_pa_t_kernel(tc, q, k, v, out):
 
         def split_ksum():
             nc.vector.tensor_reduce(out=ksum[:], in_=ksum_parts[:], axis=AXIS.X, op=ALU.add)
-            nc.vector.memset(pieces[:], 0.0)
             nc.vector.tensor_copy(out=pieces[:, :, 0], in_=ksum[:])
             nc.vector.tensor_sub(out=rest1[:], in0=ksum[:], in1=pieces[:, :, 0])
             nc.vector.tensor_copy(out=pieces[:, :, 1], in_=rest1[:])
@@ -254,6 +273,7 @@ def tile_relu_linear_att_pa_t_kernel(tc, q, k, v, out):
             nc.vector.tensor_copy(out=pieces[:, :, 2], in_=rest2[:])
 
         results = {}
+        waiting = []
 
         def output_pass(m, r, h):
             if h == 0:
@@ -271,7 +291,7 @@ def tile_relu_linear_att_pa_t_kernel(tc, q, k, v, out):
                 stop=True,
             )
             part = results[(m, r)][:, h * N_TILE : (h + 1) * N_TILE]
-            if (RANGE_BANKS * (m + r) + h) % 3 == 1:
+            if (RANGE_BANKS * (m + r) + h) % 4 == 1:
                 nc.scalar.copy(out=part, in_=num[:])
                 nc.gpsimd.tensor_mul(out=part, in0=part, in1=rden_all[:, n_cols])
             else:
@@ -293,64 +313,58 @@ def tile_relu_linear_att_pa_t_kernel(tc, q, k, v, out):
                 prepare_k(p + E_TILES)
             if is_k_tile(p + E_TILES - 1) and p + E_TILES - 1 != E_TILES - 1:
                 quantise_k(p + E_TILES - 1)
+            if is_tile(p):
+                quantise_state(p)
             if is_tile(p + 2):
                 transpose_v(p + 2)
                 if p + 2 + V_BUFS < D_TILES:
                     load_v(p + 2 + V_BUFS)
-            if is_range(p - 1):
-                spread_den(p - 1)
             if p == FIRST_STATE_ROUND:
                 quantise_v(0)
                 quantise_k(E_TILES - 1)
             if p == FIRST_STATE_ROUND + 1:
                 split_ksum()
+            if is_range(p - 1):
+                spread_den(p - 1)
+            if is_tile(p):
+                blocks = [(p, r) for r in range(min(p, Q_RANGES))]
+                if is_range(p - 1):
+                    blocks = [(m, p - 1) for m in range(p)] + blocks
+                waiting.extend([(m, r, h) for m, r in blocks for h in range(RANGE_BANKS)])
             if is_range(p):
                 regroup_q(p)
-            if is_range(p + 1):
-                relu_q(p + 1)
-            if is_tile(p):
-                quantise_state(p)
-            if is_range(p):
-                den_matmuls(p)
-                reciprocal_den(p)
-            blocks = []
-            if is_range(p - 1):
-                blocks = blocks + [(m, p - 1) for m in range(p - 1)]
-            if is_tile(p - 1):
-                blocks = blocks + [(p - 1, r) for r in range(min(p, Q_RANGES))]
-            passes = [(m, r, h) for m, r in blocks for h in range(RANGE_BANKS)]
-            share = (len(passes) + STEPS - 1) // STEPS
             if is_tile(p + 1):
+                carry = CARRY if p >= CARRY_FROM else 0
+                share = max(0, (len(waiting) - carry + STEPS - 1) // STEPS)
                 for s in range(STEPS):
                     for i in range(s * STATE_PASSES // STEPS, (s + 1) * STATE_PASSES // STEPS):
                         state_pass(p + 1, i)
-                    for m, r, h in passes[share * s : share * (s + 1)]:
-                        output_pass(m, r, h)
-                    if s == STEPS // 2 - 1 and is_tile(p + 2):
+                    for b in range(share):
+                        if waiting:
+                            output_pass(*waiting.pop(0))
+                    if s == V_QUANTISE_STEP and is_tile(p + 2):
                         quantise_v(p + 2)
+                    if s == V_SPLIT_STEP and is_tile(p + 3) and p + 3 >= FIRST_SPLIT:
+                        split_v(p + 3)
+                    if s == DEN_STEP and is_range(p):
+                        den_matmuls(p)
+                        reciprocal_den(p)
+                    if s == Q_QUANTISE_STEP and is_range(p):
+                        quantise_q(p)
                 round_state(p + 1)
-            else:
-                for m, r, h in passes:
-                    output_pass(m, r, h)
-            if is_range(p):
-                quantise_q(p)
+            elif is_tile(p):
+                while waiting:
+                    output_pass(*waiting.pop(0))
 
         with tc.tile_pool(name="k_in", bufs=3) as k_in, tc.tile_pool(name="kr", bufs=2) as kr_pool:
-            for t in range(E_TILES):
-                k_tiles[t] = k_in.tile([P, N], BF16, name="k_sb")
-                for c in range(K_PARTS):
-                    nc.sync.dma_start(
-                        out=k_tiles[t][:, c * K_PART : (c + 1) * K_PART],
-                        in_=k_rows.rearrange("(p t) n -> t p n", t=PACK)[t, :, c * K_PART : (c + 1) * K_PART],
-                    )
-            load_v(0)
-            load_v(1)
-            load_q(0)
-            for r in range(1, Q_RANGES):
-                load_q(r)
-                load_v(r + 1)
-            for m in range(Q_RANGES + 1, V_BUFS):
-                load_v(m)
+            for item in LOADS.split(" "):
+                i = int(item[1:])
+                if item[0] == "k":
+                    load_k(i, k_in)
+                elif item[0] == "v":
+                    load_v(i)
+                else:
+                    load_q(i)
             for p in range(FIRST_ROUND, 0):
                 work_round(p)
         staging = ctx.enter_context(tc.tile_pool(name="staging", bufs=STAGING_BUFS))

@@ -52,6 +52,8 @@ CARRY = 4
 CARRY_FROM = 3
 FIRST_SPLIT = 3
 LOADS = "k0 k1 k2 v0 k3 v1 v2 q0 v3 q1 v4 q2 q3 v5"
+WARM_START = 8
+WARM_K = (2, 6)
 FIRST_ROUND = -E_TILES
 FIRST_STATE_ROUND = -1
 LAST_ROUND = D_TILES - 1
@@ -79,6 +81,18 @@ def tile_relu_linear_att_pa_t_kernel(tc, q, k, v, out):
         ident_f32 = keep.tile([P, P], F32)
         make_identity(nc, ident_f32[:])
 
+        warm_w = keep.tile([P, P], BF16)
+        warm_x = keep.tile([P, N_TILE], BF16)
+        nc.vector.memset(warm_w[:], 0.0)
+        nc.vector.memset(warm_x[:], 0.0)
+        warm_ps = psum.tile([P, N_TILE], F32, tag="vk_ps", bufs=1, name="warm_ps")
+
+        def keep_warm(count):
+            for i in range(count):
+                nc.tensor.matmul(out=warm_ps[:], lhsT=warm_w[:], rhs=warm_x[:], start=True, stop=True)
+
+        keep_warm(WARM_START)
+
         k_codes = keep.tile([P, TOKEN_PASSES * E], U32, align_bytes=64)
         k_scales = keep.tile([P, TOKEN_PASSES * E], U8, align_bytes=64)
         q_codes = keep.tile([P, N], U32, align_bytes=64)
@@ -98,7 +112,7 @@ def tile_relu_linear_att_pa_t_kernel(tc, q, k, v, out):
         def new_bank(shape):
             return psum.tile(shape, F32, tag="bank", bufs=BANKS, name="bank")
 
-        def tokens_to_partitions(rows, split):
+        def tokens_to_partitions(rows, warm, split):
             words = rows[:].bitcast(F32)
             grouped = grouped_pool.tile([P, PACK * TOKEN_PASSES * P], BF16, tag="grouped", align_bytes=64)
             grouped_words = grouped[:].bitcast(F32).rearrange("p (g d u) -> p g d u", g=TOKEN_PASSES, u=PAIR)
@@ -114,6 +128,8 @@ def tile_relu_linear_att_pa_t_kernel(tc, q, k, v, out):
                             w0 = (first_pass + g) * PASS_WORDS
                             cols = slice(w0 + u, w0 + PASS_WORDS, PAIR)
                         nc.tensor.transpose(bank[:, g, u, :], words[:, cols], ident_f32[:])
+                if first_pass in warm:
+                    keep_warm(1)
                 nc.scalar.copy(
                     out=grouped_words[:, first_pass : first_pass + BANK_PASSES, :, :],
                     in_=bank[:].rearrange("p g u d -> p g d u"),
@@ -145,7 +161,7 @@ def tile_relu_linear_att_pa_t_kernel(tc, q, k, v, out):
             v_tiles[m] = v_split
 
         def transpose_v(m):
-            v_grouped[m] = tokens_to_partitions(v_tiles[m], m >= FIRST_SPLIT)
+            v_grouped[m] = tokens_to_partitions(v_tiles[m], (), m >= FIRST_SPLIT)
 
         def quantise_v(m):
             codes = v_mx.tile([P, TOKEN_PASSES * P], U32, tag="v_codes", align_bytes=64)
@@ -258,7 +274,7 @@ def tile_relu_linear_att_pa_t_kernel(tc, q, k, v, out):
                     op1=ALU.add,
                     accum_out=ksum_parts[:, t, c : c + 1],
                 )
-            k_grouped[t] = tokens_to_partitions(kr, True)
+            k_grouped[t] = tokens_to_partitions(kr, WARM_K, True)
 
         def quantise_k(t):
             cols = slice(t * TOKEN_PASSES * P, (t + 1) * TOKEN_PASSES * P)

@@ -10,6 +10,7 @@ U8 = mybir.dt.uint8
 FP8X4 = mybir.dt.float8_e4m3fn_x4
 ALU = mybir.AluOpType
 AXIS = mybir.AxisListType
+ACT = mybir.ActivationFunctionType
 
 P = 128
 PACK = 4
@@ -44,10 +45,12 @@ VK_BUFS = 2
 BANKS = 7
 STAGING_BUFS = 8
 
-V_QUANTISE_STEP = 3
+V_QUANTISE_STEP = 5
 V_SPLIT_STEP = 2
-DEN_STEP = 5
+DEN_STEP = 6
 Q_QUANTISE_STEP = 7
+FIRST_OUT = 2
+SCALAR_Q = RANGE // 8
 CARRY = 4
 CARRY_FROM = 3
 FIRST_SPLIT = 3
@@ -210,11 +213,11 @@ def tile_relu_linear_att_pa_t_kernel(tc, q, k, v, out):
 
         def regroup_q(r):
             grouped = grouped_pool.tile([P, PACK * RANGE], BF16, tag="grouped", align_bytes=64)
-            nc.vector.tensor_scalar_max(
-                out=grouped[:].rearrange("p (c i t) -> p c t i", i=RUN, t=PACK),
-                in0=q_ranges[r][:].rearrange("p t (c i) -> p c t i", i=RUN),
-                scalar1=0.0,
-            )
+            cut = RANGE - SCALAR_Q
+            dst = grouped[:].rearrange("p (c i t) -> p c t i", i=RUN, t=PACK)
+            src = q_ranges[r][:].rearrange("p t (c i) -> p c t i", i=RUN)
+            nc.vector.tensor_scalar_max(out=dst[:, : cut // RUN], in0=src[:, : cut // RUN], scalar1=0.0)
+            nc.scalar.activation(out=dst[:, cut // RUN :], in_=src[:, cut // RUN :], func=ACT.Relu)
             q_grouped[r] = grouped
 
         def quantise_q(r):
@@ -289,6 +292,7 @@ def tile_relu_linear_att_pa_t_kernel(tc, q, k, v, out):
             nc.vector.tensor_copy(out=pieces[:, :, 2], in_=rest2[:])
 
         results = {}
+        emitted = [0]
         waiting = []
 
         def output_pass(m, r, h):
@@ -307,7 +311,8 @@ def tile_relu_linear_att_pa_t_kernel(tc, q, k, v, out):
                 stop=True,
             )
             part = results[(m, r)][:, h * N_TILE : (h + 1) * N_TILE]
-            if (RANGE_BANKS * (m + r) + h) % 4 == 1:
+            emitted[0] += 1
+            if emitted[0] % 4 == 1:
                 nc.scalar.copy(out=part, in_=num[:])
                 nc.gpsimd.tensor_mul(out=part, in0=part, in1=rden_all[:, n_cols])
             else:
@@ -352,6 +357,9 @@ def tile_relu_linear_att_pa_t_kernel(tc, q, k, v, out):
             if is_tile(p + 1):
                 carry = CARRY if p >= CARRY_FROM else 0
                 share = max(0, (len(waiting) - carry + STEPS - 1) // STEPS)
+                if not is_tile(p + 2):
+                    for b in range(min(FIRST_OUT, len(waiting))):
+                        output_pass(*waiting.pop(0))
                 for s in range(STEPS):
                     for i in range(s * STATE_PASSES // STEPS, (s + 1) * STATE_PASSES // STEPS):
                         state_pass(p + 1, i)

@@ -45,7 +45,7 @@ VK_BUFS = 2
 BANKS = 7
 STAGING_BUFS = 8
 
-V_QUANTISE_STEP = 5
+V_QUANTISE_STEP = 4
 V_SPLIT_STEP = 2
 DEN_STEP = 6
 Q_QUANTISE_STEP = 7
@@ -292,11 +292,10 @@ def tile_relu_linear_att_pa_t_kernel(tc, q, k, v, out):
             nc.vector.tensor_copy(out=pieces[:, :, 2], in_=rest2[:])
 
         results = {}
-        emitted = [0]
         waiting = []
 
-        def output_pass(m, r, h):
-            if h == 0:
+        def output_pass(m, r, h, by_pool):
+            if (m, r) not in results:
                 results[(m, r)] = staging.tile([P, RANGE], F32, tag="result", name="result")
             d_cols = slice(m * P, (m + 1) * P)
             n_cols = slice(r * RANGE + h * N_TILE, r * RANGE + (h + 1) * N_TILE)
@@ -311,8 +310,7 @@ def tile_relu_linear_att_pa_t_kernel(tc, q, k, v, out):
                 stop=True,
             )
             part = results[(m, r)][:, h * N_TILE : (h + 1) * N_TILE]
-            emitted[0] += 1
-            if emitted[0] % 4 == 1:
+            if by_pool:
                 nc.scalar.copy(out=part, in_=num[:])
                 nc.gpsimd.tensor_mul(out=part, in0=part, in1=rden_all[:, n_cols])
             else:
@@ -351,7 +349,10 @@ def tile_relu_linear_att_pa_t_kernel(tc, q, k, v, out):
                 blocks = [(p, r) for r in range(min(p, Q_RANGES))]
                 if is_range(p - 1):
                     blocks = [(m, p - 1) for m in range(p)] + blocks
-                waiting.extend([(m, r, h) for m, r in blocks for h in range(RANGE_BANKS)])
+                for i in range(0, len(blocks), 2):
+                    m, r = blocks[i]
+                    other = [(b[0], b[1], h, False) for b in blocks[i + 1 : i + 2] for h in range(RANGE_BANKS)]
+                    waiting.extend([(m, r, 0, len(other) > 0)] + other + [(m, r, 1, False)])
             if is_range(p):
                 regroup_q(p)
             if is_tile(p + 1):

@@ -26,8 +26,7 @@ PASS_WORDS = K_PASS // PAIR
 BANK_PASSES = 2
 N_TILE = 512
 K_PARTS = 2
-K_PART = N // K_PARTS
-PART_PASSES = TOKEN_PASSES // K_PARTS
+FIRST_K_PARTS = 4
 Q_RANGES = 4
 RANGE = N // Q_RANGES
 RANGE_TILES = RANGE // P
@@ -55,7 +54,7 @@ CARRY = 4
 CARRY_FROM = 3
 FIRST_SPLIT = 3
 LOADS = "k0 k1 k2 v0 k3 v1 v2 q0 v3 q1 v4 q2 q3 v5"
-WARM_START = 8
+WARM_START = 6
 WARM_K = (2, 6)
 FIRST_ROUND = -E_TILES
 FIRST_STATE_ROUND = -1
@@ -104,7 +103,7 @@ def tile_relu_linear_att_pa_t_kernel(tc, q, k, v, out):
         vk_scales = keep.tile([P, DV], U8, align_bytes=64)
         q_ranges = [keep.tile([P, E_TILES, RANGE], BF16, name="q_sb%d" % r) for r in range(Q_RANGES)]
         rden_all = keep.tile([P, N], F32)
-        ksum_parts = keep.tile([P, E_TILES, K_PARTS], F32)
+        ksum_parts = keep.tile([P, E_TILES, FIRST_K_PARTS], F32)
         ksum = keep.tile([P, E_TILES], F32)
         pieces = keep.tile([P, E_TILES, DEN_COLS], BF16)
         rest1 = keep.tile([P, E_TILES], F32)
@@ -124,8 +123,9 @@ def tile_relu_linear_att_pa_t_kernel(tc, q, k, v, out):
                 for g in range(BANK_PASSES):
                     for u in range(PAIR):
                         if split:
-                            part, g_part = divmod(first_pass + g, PART_PASSES)
-                            w0 = (part * PAIR + u) * PART_PASSES * P + g_part * P
+                            part_passes = TOKEN_PASSES // split
+                            part, g_part = divmod(first_pass + g, part_passes)
+                            w0 = (part * PAIR + u) * part_passes * P + g_part * P
                             cols = slice(w0, w0 + P)
                         else:
                             w0 = (first_pass + g) * PASS_WORDS
@@ -140,6 +140,7 @@ def tile_relu_linear_att_pa_t_kernel(tc, q, k, v, out):
             return grouped
 
         nc.vector.memset(pieces[:], 0.0)
+        nc.vector.memset(ksum_parts[:], 0.0)
 
         v_tiles = {}
         v_grouped = {}
@@ -164,7 +165,7 @@ def tile_relu_linear_att_pa_t_kernel(tc, q, k, v, out):
             v_tiles[m] = v_split
 
         def transpose_v(m):
-            v_grouped[m] = tokens_to_partitions(v_tiles[m], (), m >= FIRST_SPLIT)
+            v_grouped[m] = tokens_to_partitions(v_tiles[m], (), K_PARTS if m >= FIRST_SPLIT else 0)
 
         def quantise_v(m):
             codes = v_mx.tile([P, TOKEN_PASSES * P], U32, tag="v_codes", align_bytes=64)
@@ -256,18 +257,24 @@ def tile_relu_linear_att_pa_t_kernel(tc, q, k, v, out):
         k_tiles = {}
         k_grouped = {}
 
+        def k_parts(t):
+            return FIRST_K_PARTS if t == 0 else K_PARTS
+
         def load_k(t, k_in):
             k_tiles[t] = k_in.tile([P, N], BF16, name="k_sb")
-            for c in range(K_PARTS):
+            parts = k_parts(t)
+            for c in range(parts):
+                cols = slice(c * N // parts, (c + 1) * N // parts)
                 nc.sync.dma_start(
-                    out=k_tiles[t][:, c * K_PART : (c + 1) * K_PART],
-                    in_=k_rows.rearrange("(p t) n -> t p n", t=PACK)[t, :, c * K_PART : (c + 1) * K_PART],
+                    out=k_tiles[t][:, cols],
+                    in_=k_rows.rearrange("(p t) n -> t p n", t=PACK)[t, :, cols],
                 )
 
         def prepare_k(t):
             kr = kr_pool.tile([P, N], BF16, name="kr")
-            for c in range(K_PARTS):
-                part = slice(c * K_PART, (c + 1) * K_PART)
+            parts = k_parts(t)
+            for c in range(parts):
+                part = slice(c * N // parts, (c + 1) * N // parts)
                 nc.vector.tensor_scalar(
                     out=kr[:, part].rearrange("p (u w y) -> p u w y", u=PAIR, y=PAIR),
                     in0=k_tiles[t][:, part].rearrange("p (w u y) -> p u w y", u=PAIR, y=PAIR),
@@ -277,7 +284,7 @@ def tile_relu_linear_att_pa_t_kernel(tc, q, k, v, out):
                     op1=ALU.add,
                     accum_out=ksum_parts[:, t, c : c + 1],
                 )
-            k_grouped[t] = tokens_to_partitions(kr, WARM_K, True)
+            k_grouped[t] = tokens_to_partitions(kr, WARM_K, parts)
 
         def quantise_k(t):
             cols = slice(t * TOKEN_PASSES * P, (t + 1) * TOKEN_PASSES * P)

from contextlib import ExitStack

import concourse.mybir as mybir
from concourse.masks import make_identity

F32 = mybir.dt.float32
BF16 = mybir.dt.bfloat16
U32 = mybir.dt.uint32
U8 = mybir.dt.uint8
FP8X4 = mybir.dt.float8_e4m3fn_x4
ALU = mybir.AluOpType
AXIS = mybir.AxisListType
ACT = mybir.ActivationFunctionType

P = 128
PACK = 4
K_PASS = P * PACK
E = 512
DV = 1024
N = 4096
E_TILES = E // P
D_TILES = DV // P
TOKEN_PASSES = N // K_PASS
PAIR = 2
PASS_WORDS = K_PASS // PAIR
BANK_PASSES = 2
N_TILE = 512
K_PARTS = 2
FIRST_K_PARTS = 4
Q_RANGES = 4
RANGE = N // Q_RANGES
RANGE_TILES = RANGE // P
RANGE_BANKS = RANGE // N_TILE
RUN = 4
STATE_PASSES = E_TILES * TOKEN_PASSES
STEPS = 8
KSUM_PIECES = 3
DEN_COLS = 32

V_BUFS = 6
GROUPED_BUFS = 3
V_MX_BUFS = 2
VK_BUFS = 2
BANKS = 7
STAGING_BUFS = 8

V_QUANTISE_STEP = 4
V_SPLIT_STEP = 2
DEN_STEP = 6
Q_QUANTISE_STEP = 7
FIRST_OUT = 2
SCALAR_Q = RANGE // 8
CARRY = 4
CARRY_FROM = 3
FIRST_SPLIT = 3
LOADS = "k0 k1 k2 v0 k3 v1 v2 q0 v3 q1 v4 q2 q3 v5"
WARM_START = 6
WARM_K = (2, 6)
FIRST_ROUND = -E_TILES
FIRST_STATE_ROUND = -1
LAST_ROUND = D_TILES - 1

FLOPS = 2 * DV * E * N * 2 + 2 * E * N


def tile_relu_linear_att_pa_t_kernel(tc, q, k, v, out):
    nc = tc.nc
    q_rows = q.rearrange("b h e n -> (b h e) n")
    k_rows = k.rearrange("b h e n -> (b h e) n")
    v_rows = v.rearrange("b h d n -> (b h d) n")
    out_rows = out.rearrange("b (d x) c -> (b d) (x c)", x=N // DV)

    with ExitStack() as ctx:
        ctx.enter_context(tc.manual_schedule())
        keep = ctx.enter_context(tc.tile_pool(name="keep", bufs=1))
        v_in = ctx.enter_context(tc.tile_pool(name="v_in", bufs=V_BUFS))
        grouped_pool = ctx.enter_context(tc.tile_pool(name="grouped", bufs=GROUPED_BUFS))
        v_mx = ctx.enter_context(tc.tile_pool(name="v_mx", bufs=V_MX_BUFS))
        split_pool = ctx.enter_context(tc.tile_pool(name="split", bufs=2))
        vk_pool = ctx.enter_context(tc.tile_pool(name="vk", bufs=VK_BUFS))
        psum = ctx.enter_context(tc.psum_pool(name="psum", bufs=1))

        ident_f32 = keep.tile([P, P], F32)
        make_identity(nc, ident_f32[:])

        warm_w = keep.tile([P, P], BF16)
        warm_x = keep.tile([P, N_TILE], BF16)
        nc.vector.memset(warm_w[:], 0.0)
        nc.vector.memset(warm_x[:], 0.0)
        warm_ps = psum.tile([P, N_TILE], F32, tag="vk_ps", bufs=1, name="warm_ps")

        def keep_warm(count):
            for i in range(count):
                nc.tensor.matmul(out=warm_ps[:], lhsT=warm_w[:], rhs=warm_x[:], start=True, stop=True)

        keep_warm(WARM_START)

        k_codes = keep.tile([P, TOKEN_PASSES * E], U32, align_bytes=64)
        k_scales = keep.tile([P, TOKEN_PASSES * E], U8, align_bytes=64)
        q_codes = keep.tile([P, N], U32, align_bytes=64)
        q_scales = keep.tile([P, N], U8, align_bytes=64)
        vk_codes = keep.tile([P, DV], U32, align_bytes=64)
        vk_scales = keep.tile([P, DV], U8, align_bytes=64)
        q_ranges = [keep.tile([P, E_TILES, RANGE], BF16, name="q_sb%d" % r) for r in range(Q_RANGES)]
        rden_all = keep.tile([P, N], F32)
        ksum_parts = keep.tile([P, E_TILES, FIRST_K_PARTS], F32)
        ksum = keep.tile([P, E_TILES], F32)
        pieces = keep.tile([P, E_TILES, DEN_COLS], BF16)
        rest1 = keep.tile([P, E_TILES], F32)
        rest2 = keep.tile([P, E_TILES], F32)
        den = keep.tile([P, Q_RANGES, RANGE_TILES], F32)
        rden = keep.tile([P, Q_RANGES, RANGE_TILES], F32)

        def new_bank(shape):
            return psum.tile(shape, F32, tag="bank", bufs=BANKS, name="bank")

        def tokens_to_partitions(rows, warm, split):
            words = rows[:].bitcast(F32)
            grouped = grouped_pool.tile([P, PACK * TOKEN_PASSES * P], BF16, tag="grouped", align_bytes=64)
            grouped_words = grouped[:].bitcast(F32).rearrange("p (g d u) -> p g d u", g=TOKEN_PASSES, u=PAIR)
            for first_pass in range(0, TOKEN_PASSES, BANK_PASSES):
                bank = new_bank([P, BANK_PASSES, PAIR, P])
                for g in range(BANK_PASSES):
                    for u in range(PAIR):
                        if split:
                            part_passes = TOKEN_PASSES // split
                            part, g_part = divmod(first_pass + g, part_passes)
                            w0 = (part * PAIR + u) * part_passes * P + g_part * P
                            cols = slice(w0, w0 + P)
                        else:
                            w0 = (first_pass + g) * PASS_WORDS
                            cols = slice(w0 + u, w0 + PASS_WORDS, PAIR)
                        nc.tensor.transpose(bank[:, g, u, :], words[:, cols], ident_f32[:])
                if first_pass in warm:
                    keep_warm(1)
                nc.scalar.copy(
                    out=grouped_words[:, first_pass : first_pass + BANK_PASSES, :, :],
                    in_=bank[:].rearrange("p g u d -> p g d u"),
                )
            return grouped

        nc.vector.memset(pieces[:], 0.0)
        nc.vector.memset(ksum_parts[:], 0.0)

        v_tiles = {}
        v_grouped = {}
        v_quantised = {}
        vk_sums = {}
        vk_rounded = {}

        def load_v(m):
            v_sb = v_in.tile([P, N], BF16, name="v_sb")
            nc.sync.dma_start(out=v_sb[:], in_=v_rows[m * P : (m + 1) * P, :])
            v_tiles[m] = v_sb

        def split_v(m):
            v_sb = v_tiles[m]
            v_split = split_pool.tile([P, N], BF16, name="v_split")
            for c in range(K_PARTS):
                part = slice(c * (N // PAIR) // K_PARTS, (c + 1) * (N // PAIR) // K_PARTS)
                nc.scalar.copy(
                    out=v_split[:].bitcast(F32)[:, part].rearrange("p (u w) -> p u w", u=PAIR),
                    in_=v_sb[:].bitcast(F32)[:, part].rearrange("p (w u) -> p u w", u=PAIR),
                )
            v_tiles[m] = v_split

        def transpose_v(m):
            v_grouped[m] = tokens_to_partitions(v_tiles[m], (), K_PARTS if m >= FIRST_SPLIT else 0)

        def quantise_v(m):
            codes = v_mx.tile([P, TOKEN_PASSES * P], U32, tag="v_codes", align_bytes=64)
            scales = v_mx.tile([P, TOKEN_PASSES * P], U8, tag="v_scales", align_bytes=64)
            nc.vector.quantize_mx(out=codes[:].bitcast(FP8X4), scales=scales[:], in_=v_grouped[m][:])
            v_quantised[m] = (codes, scales)

        def state_pass(m, i):
            t = i // TOKEN_PASSES
            g = i % TOKEN_PASSES
            if i == 0:
                vk_sums[m] = psum.tile([P, E_TILES, P], F32, tag="vk_ps", bufs=1, name="vk_ps")
            codes, scales = v_quantised[m]
            e_cols = slice((t * TOKEN_PASSES + g) * P, (t * TOKEN_PASSES + g + 1) * P)
            nc.tensor.matmul_mx(
                out=vk_sums[m][:, t, :],
                lhsT=k_codes[:, e_cols].bitcast(FP8X4),
                lhsT_scale=k_scales[:, e_cols],
                rhs=codes[:, g * P : (g + 1) * P].bitcast(FP8X4),
                rhs_scale=scales[:, g * P : (g + 1) * P],
                start=(g == 0),
                stop=(g == TOKEN_PASSES - 1),
            )

        def round_state(m):
            vk_grouped = vk_pool.tile([P, P, PACK], BF16, tag="vk_grouped", align_bytes=64)
            nc.scalar.copy(out=vk_grouped[:], in_=vk_sums[m][:].rearrange("p t d -> p d t"))
            vk_rounded[m] = vk_grouped

        def quantise_state(m):
            cols = slice(m * P, (m + 1) * P)
            nc.vector.quantize_mx(
                out=vk_codes[:, cols].bitcast(FP8X4),
                scales=vk_scales[:, cols],
                in_=vk_rounded[m][:].rearrange("p d t -> p (d t)"),
            )

        q_grouped = {}
        den_sums = {}

        def load_q(r):
            nc.sync.dma_start(
                out=q_ranges[r][:],
                in_=q_rows.rearrange("(p t) n -> p t n", t=PACK)[:, :, r * RANGE : (r + 1) * RANGE],
            )

        def regroup_q(r):
            grouped = grouped_pool.tile([P, PACK * RANGE], BF16, tag="grouped", align_bytes=64)
            cut = RANGE - SCALAR_Q
            dst = grouped[:].rearrange("p (c i t) -> p c t i", i=RUN, t=PACK)
            src = q_ranges[r][:].rearrange("p t (c i) -> p c t i", i=RUN)
            nc.vector.tensor_scalar_max(out=dst[:, : cut // RUN], in0=src[:, : cut // RUN], scalar1=0.0)
            nc.scalar.activation(out=dst[:, cut // RUN :], in_=src[:, cut // RUN :], func=ACT.Relu)
            q_grouped[r] = grouped

        def quantise_q(r):
            cols = slice(r * RANGE, (r + 1) * RANGE)
            nc.vector.quantize_mx(out=q_codes[:, cols].bitcast(FP8X4), scales=q_scales[:, cols], in_=q_grouped[r][:])

        def den_matmuls(r):
            den_ps = new_bank([P, RANGE_TILES, DEN_COLS])
            grouped = q_grouped[r][:].rearrange("p (n t) -> p n t", t=PACK)
            for j in range(RANGE_TILES):
                for t in range(E_TILES):
                    nc.tensor.matmul(
                        out=den_ps[:, j, :],
                        lhsT=grouped[:, j * P : (j + 1) * P, t],
                        rhs=pieces[:, t, :],
                        start=(t == 0),
                        stop=(t == E_TILES - 1),
                    )
            den_sums[r] = den_ps

        def reciprocal_den(r):
            nc.vector.tensor_reduce(out=den[:, r, :], in_=den_sums[r][:, :, 0:KSUM_PIECES], axis=AXIS.X, op=ALU.add)
            nc.vector.reciprocal(out=rden[:, r, :], in_=den[:, r, :])

        def spread_den(r):
            for h in range(RANGE_BANKS):
                bank = new_bank([P, N_TILE // P, P])
                for square in range(N_TILE // P):
                    j = h * (N_TILE // P) + square
                    nc.tensor.transpose(
                        bank[:, square, :], rden[:, r, j : j + 1].to_broadcast([P, P]), ident_f32[:]
                    )
                first = r * RANGE + h * N_TILE
                nc.scalar.copy(out=rden_all[:, first : first + N_TILE], in_=bank[:].rearrange("p i c -> p (i c)"))

        k_tiles = {}
        k_grouped = {}

        def k_parts(t):
            return FIRST_K_PARTS if t == 0 else K_PARTS

        def load_k(t, k_in):
            k_tiles[t] = k_in.tile([P, N], BF16, name="k_sb")
            parts = k_parts(t)
            for c in range(parts):
                cols = slice(c * N // parts, (c + 1) * N // parts)
                nc.sync.dma_start(
                    out=k_tiles[t][:, cols],
                    in_=k_rows.rearrange("(p t) n -> t p n", t=PACK)[t, :, cols],
                )

        def prepare_k(t):
            kr = kr_pool.tile([P, N], BF16, name="kr")
            parts = k_parts(t)
            for c in range(parts):
                part = slice(c * N // parts, (c + 1) * N // parts)
                nc.vector.tensor_scalar(
                    out=kr[:, part].rearrange("p (u w y) -> p u w y", u=PAIR, y=PAIR),
                    in0=k_tiles[t][:, part].rearrange("p (w u y) -> p u w y", u=PAIR, y=PAIR),
                    scalar1=0.0,
                    scalar2=None,
                    op0=ALU.max,
                    op1=ALU.add,
                    accum_out=ksum_parts[:, t, c : c + 1],
                )
            k_grouped[t] = tokens_to_partitions(kr, WARM_K, parts)

        def quantise_k(t):
            cols = slice(t * TOKEN_PASSES * P, (t + 1) * TOKEN_PASSES * P)
            nc.vector.quantize_mx(out=k_codes[:, cols].bitcast(FP8X4), scales=k_scales[:, cols], in_=k_grouped[t][:])

        def split_ksum():
            nc.vector.tensor_reduce(out=ksum[:], in_=ksum_parts[:], axis=AXIS.X, op=ALU.add)
            nc.vector.tensor_copy(out=pieces[:, :, 0], in_=ksum[:])
            nc.vector.tensor_sub(out=rest1[:], in0=ksum[:], in1=pieces[:, :, 0])
            nc.vector.tensor_copy(out=pieces[:, :, 1], in_=rest1[:])
            nc.vector.tensor_sub(out=rest2[:], in0=rest1[:], in1=pieces[:, :, 1])
            nc.vector.tensor_copy(out=pieces[:, :, 2], in_=rest2[:])

        results = {}
        waiting = []

        def output_pass(m, r, h, by_pool):
            if (m, r) not in results:
                results[(m, r)] = staging.tile([P, RANGE], F32, tag="result", name="result")
            d_cols = slice(m * P, (m + 1) * P)
            n_cols = slice(r * RANGE + h * N_TILE, r * RANGE + (h + 1) * N_TILE)
            num = new_bank([P, N_TILE])
            nc.tensor.matmul_mx(
                out=num[:],
                lhsT=vk_codes[:, d_cols].bitcast(FP8X4),
                lhsT_scale=vk_scales[:, d_cols],
                rhs=q_codes[:, n_cols].bitcast(FP8X4),
                rhs_scale=q_scales[:, n_cols],
                start=True,
                stop=True,
            )
            part = results[(m, r)][:, h * N_TILE : (h + 1) * N_TILE]
            if by_pool:
                nc.scalar.copy(out=part, in_=num[:])
                nc.gpsimd.tensor_mul(out=part, in0=part, in1=rden_all[:, n_cols])
            else:
                nc.vector.tensor_mul(out=part, in0=num[:], in1=rden_all[:, n_cols])
            if h == RANGE_BANKS - 1:
                nc.sync.dma_start(out=out_rows[d_cols, r * RANGE : (r + 1) * RANGE], in_=results[(m, r)][:])

        def is_k_tile(t):
            return 0 <= t < E_TILES

        def is_tile(m):
            return 0 <= m < D_TILES

        def is_range(r):
            return 0 <= r < Q_RANGES

        def work_round(p):
            if is_k_tile(p + E_TILES):
                prepare_k(p + E_TILES)
            if is_k_tile(p + E_TILES - 1) and p + E_TILES - 1 != E_TILES - 1:
                quantise_k(p + E_TILES - 1)
            if is_tile(p):
                quantise_state(p)
            if is_tile(p + 2):
                transpose_v(p + 2)
                if p + 2 + V_BUFS < D_TILES:
                    load_v(p + 2 + V_BUFS)
            if p == FIRST_STATE_ROUND:
                quantise_v(0)
                quantise_k(E_TILES - 1)
            if p == FIRST_STATE_ROUND + 1:
                split_ksum()
            if is_range(p - 1):
                spread_den(p - 1)
            if is_tile(p):
                blocks = [(p, r) for r in range(min(p, Q_RANGES))]
                if is_range(p - 1):
                    blocks = [(m, p - 1) for m in range(p)] + blocks
                for i in range(0, len(blocks), 2):
                    m, r = blocks[i]
                    other = [(b[0], b[1], h, False) for b in blocks[i + 1 : i + 2] for h in range(RANGE_BANKS)]
                    waiting.extend([(m, r, 0, len(other) > 0)] + other + [(m, r, 1, False)])
            if is_range(p):
                regroup_q(p)
            if is_tile(p + 1):
                carry = CARRY if p >= CARRY_FROM else 0
                share = max(0, (len(waiting) - carry + STEPS - 1) // STEPS)
                if not is_tile(p + 2):
                    for b in range(min(FIRST_OUT, len(waiting))):
                        output_pass(*waiting.pop(0))
                for s in range(STEPS):
                    for i in range(s * STATE_PASSES // STEPS, (s + 1) * STATE_PASSES // STEPS):
                        state_pass(p + 1, i)
                    for b in range(share):
                        if waiting:
                            output_pass(*waiting.pop(0))
                    if s == V_QUANTISE_STEP and is_tile(p + 2):
                        quantise_v(p + 2)
                    if s == V_SPLIT_STEP and is_tile(p + 3) and p + 3 >= FIRST_SPLIT:
                        split_v(p + 3)
                    if s == DEN_STEP and is_range(p):
                        den_matmuls(p)
                        reciprocal_den(p)
                    if s == Q_QUANTISE_STEP and is_range(p):
                        quantise_q(p)
                round_state(p + 1)
            elif is_tile(p):
                while waiting:
                    output_pass(*waiting.pop(0))

        with tc.tile_pool(name="k_in", bufs=3) as k_in, tc.tile_pool(name="kr", bufs=2) as kr_pool:
            for item in LOADS.split(" "):
                i = int(item[1:])
                if item[0] == "k":
                    load_k(i, k_in)
                elif item[0] == "v":
                    load_v(i)
                else:
                    load_q(i)
            for p in range(FIRST_ROUND, 0):
                work_round(p)
        staging = ctx.enter_context(tc.tile_pool(name="staging", bufs=STAGING_BUFS))
        for p in range(0, LAST_ROUND + 1):
            work_round(p)
